import numpy as np
import ml_dtypes

BF16 = ml_dtypes.bfloat16


def bf(x):
    return np.asarray(x, np.float32).astype(BF16)


def f32(x):
    return np.asarray(x, np.float32)


def f64(x):
    return np.asarray(x).astype(np.float64)


def striped(idx):
    return np.tile(idx.reshape(-1, 16).T, (8, 1))


D, S, N, M, CH = 128, 1024, 128, 128, 16
E = CH * CH
BETA = 0.5


def setup_inputs():
    amp = 0.05 + 0.2 * np.random.random((1, N))
    return {"k_store": bf(np.random.standard_normal((D, S))), "pq": bf(np.random.standard_normal((D, M))), "cov": f32(np.random.standard_normal((E, N)) * amp), "v": bf(np.random.standard_normal((N, D))), "offs": striped(np.random.permutation(S)[:N])}


def reference(k_store, pq, cov, v, offs):
    idx = offs[:16].T.reshape(-1)
    score = f64(pq).T @ f64(k_store)[:, idx]
    dist = np.sqrt(np.sum(f64(cov) ** 2, axis=0, keepdims=True))
    z = score / np.sqrt(D) - BETA * dist
    ex = np.exp(z - z.max(axis=1, keepdims=True))
    a = ex / ex.sum(axis=1, keepdims=True)
    return a @ f64(v)

@@ -1,0 +1,74 @@
+import math
+
+import concourse.mybir as mybir
+from concourse.masks import make_identity
+
+BF16, F32, U16 = mybir.dt.bfloat16, mybir.dt.float32, mybir.dt.uint16
+ALU = mybir.AluOpType
+ACT = mybir.ActivationFunctionType
+
+P = 128
+S = 1024
+N = 128
+COV_BLOCKS = 2
+BETA = 0.5
+
+FLOPS = 2 * P * P * N + 2 * COV_BLOCKS * P * N + 2 * P * N * P
+
+
+def tile_riemannianlunatemporalcompression_kernel(tc, k_store, pq, cov, v, offs, out):
+    nc = tc.nc
+    with (
+        tc.tile_pool(name="held", bufs=1) as held,
+        tc.psum_pool(name="psum", bufs=1) as psum,
+    ):
+        offsets = held.tile([P, N // 16], U16, name="offsets")
+        nc.sync.dma_start(offsets[:], offs)
+        cov_rows = held.tile([P, COV_BLOCKS, N], F32, name="cov_rows")
+        nc.scalar.dma_start(cov_rows[:], cov.rearrange("(b p) j -> p b j", p=P))
+        keys = held.tile([P, S], BF16, name="keys")
+        nc.sync.dma_start(keys[:], k_store)
+        queries = held.tile([P, P], BF16, name="queries")
+        nc.scalar.dma_start(queries[:], pq)
+        values = held.tile([P, P], BF16, name="values")
+        nc.gpsimd.dma_start(values[:], v)
+
+        ones = held.tile([P, P], BF16, name="ones")
+        nc.vector.memset(ones[:], 1.0)
+        identity = held.tile([P, P], BF16, name="identity")
+        make_identity(nc, identity[:])
+
+        squares = held.tile([P, COV_BLOCKS, N], BF16, name="squares")
+        nc.vector.tensor_tensor(squares[:], cov_rows[:], cov_rows[:], ALU.mult)
+        sumsq = psum.tile([P, N], F32, name="sumsq")
+        for b in range(COV_BLOCKS):
+            nc.tensor.matmul(
+                sumsq[:], ones[:], squares[:, b, :], start=(b == 0), stop=(b == COV_BLOCKS - 1)
+            )
+        half_dist = held.tile([P, N], F32, name="half_dist")
+        nc.scalar.activation(half_dist[:], sumsq[:], ACT.Sqrt, scale=BETA * BETA)
+
+        score = psum.tile([P, N], F32, name="score")
+        nc.tensor.matmul(score[:], queries[:], keys[:].indirect(offsets[:]), start=True, stop=True)
+
+        z = held.tile([P, N], F32, name="z")
+        nc.vector.scalar_tensor_tensor(
+            z[:], score[:], 1.0 / math.sqrt(P), half_dist[:], op0=ALU.mult, op1=ALU.subtract
+        )
+        neg_max = held.tile([P, 1], F32, name="neg_max")
+        nc.vector.tensor_reduce(neg_max[:], z[:], mybir.AxisListType.X, ALU.max, negate=True)
+        weights = held.tile([P, N], BF16, name="weights")
+        row_sum = held.tile([P, 1], F32, name="row_sum")
+        nc.scalar.activation(weights[:], z[:], ACT.Exp, bias=neg_max[:], accum_out=row_sum[:])
+        inv_sum = held.tile([P, 1], F32, name="inv_sum")
+        nc.vector.reciprocal(inv_sum[:], row_sum[:])
+
+        weights_t_psum = psum.tile([P, P], BF16, name="weights_t_psum")
+        nc.tensor.transpose(weights_t_psum[:], weights[:], identity[:])
+        weights_t = held.tile([P, P], BF16, name="weights_t")
+        nc.vector.tensor_copy(weights_t[:], weights_t_psum[:])
+        packed = psum.tile([P, P], F32, name="packed")
+        nc.tensor.matmul(packed[:], weights_t[:], values[:], start=True, stop=True)
+        result = held.tile([P, P], F32, name="result")
+        nc.vector.tensor_scalar(result[:], packed[:], inv_sum[:], None, op0=ALU.mult)
+        nc.sync.dma_start(out, result[:])

@@ -22,21 +22,23 @@ def tile_riemannianlunatemporalcompression_kernel(tc, k_store, pq, cov, v, offs,
         tc.tile_pool(name="held", bufs=1) as held,
         tc.psum_pool(name="psum", bufs=1) as psum,
     ):
+        cov_rows = held.tile([P, COV_BLOCKS, N], F32, name="cov_rows")
+        nc.sync.dma_start(cov_rows[:], cov.rearrange("(p b) j -> p b j", b=COV_BLOCKS))
+        keys = held.tile([P, S], BF16, name="keys")
+        nc.scalar.dma_start(keys[:], k_store)
         offsets = held.tile([P, N // 16], U16, name="offsets")
         nc.sync.dma_start(offsets[:], offs)
-        cov_rows = held.tile([P, COV_BLOCKS, N], F32, name="cov_rows")
-        nc.scalar.dma_start(cov_rows[:], cov.rearrange("(b p) j -> p b j", p=P))
-        keys = held.tile([P, S], BF16, name="keys")
-        nc.sync.dma_start(keys[:], k_store)
         queries = held.tile([P, P], BF16, name="queries")
         nc.scalar.dma_start(queries[:], pq)
-        values = held.tile([P, P], BF16, name="values")
-        nc.gpsimd.dma_start(values[:], v)
 
         ones = held.tile([P, P], BF16, name="ones")
         nc.vector.memset(ones[:], 1.0)
-        identity = held.tile([P, P], BF16, name="identity")
+        identity = held.tile([P, P], F32, name="identity")
         make_identity(nc, identity[:])
+
+        values_and_one = held.tile([P, P + 1], BF16, name="values_and_one")
+        nc.gpsimd.dma_start(values_and_one[:, 0:P], v)
+        nc.vector.memset(values_and_one[:, P : P + 1], 1.0)
 
         squares = held.tile([P, COV_BLOCKS, N], BF16, name="squares")
         nc.vector.tensor_tensor(squares[:], cov_rows[:], cov_rows[:], ALU.mult)
@@ -55,20 +57,20 @@ def tile_riemannianlunatemporalcompression_kernel(tc, k_store, pq, cov, v, offs,
         nc.vector.scalar_tensor_tensor(
             z[:], score[:], 1.0 / math.sqrt(P), half_dist[:], op0=ALU.mult, op1=ALU.subtract
         )
-        neg_max = held.tile([P, 1], F32, name="neg_max")
-        nc.vector.tensor_reduce(neg_max[:], z[:], mybir.AxisListType.X, ALU.max, negate=True)
-        weights = held.tile([P, N], BF16, name="weights")
-        row_sum = held.tile([P, 1], F32, name="row_sum")
-        nc.scalar.activation(weights[:], z[:], ACT.Exp, bias=neg_max[:], accum_out=row_sum[:])
-        inv_sum = held.tile([P, 1], F32, name="inv_sum")
-        nc.vector.reciprocal(inv_sum[:], row_sum[:])
+        row_max = held.tile([P, 1], F32, name="row_max")
+        nc.vector.tensor_reduce(row_max[:], z[:], mybir.AxisListType.X, ALU.max)
+        shifted = held.tile([P, N], F32, name="shifted")
+        nc.vector.tensor_scalar(shifted[:], z[:], row_max[:], None, op0=ALU.subtract)
 
-        weights_t_psum = psum.tile([P, P], BF16, name="weights_t_psum")
-        nc.tensor.transpose(weights_t_psum[:], weights[:], identity[:])
+        shifted_t = psum.tile([P, P], F32, name="shifted_t")
+        nc.tensor.transpose(shifted_t[:], shifted[:], identity[:])
         weights_t = held.tile([P, P], BF16, name="weights_t")
-        nc.vector.tensor_copy(weights_t[:], weights_t_psum[:])
-        packed = psum.tile([P, P], F32, name="packed")
-        nc.tensor.matmul(packed[:], weights_t[:], values[:], start=True, stop=True)
+        nc.scalar.activation(weights_t[:], shifted_t[:], ACT.Exp)
+
+        packed = psum.tile([P, P + 1], F32, name="packed")
+        nc.tensor.matmul(packed[:], weights_t[:], values_and_one[:], start=True, stop=True)
+        inv_sum = held.tile([P, 1], F32, name="inv_sum")
+        nc.vector.reciprocal(inv_sum[:], packed[:, P : P + 1])
         result = held.tile([P, P], F32, name="result")
-        nc.vector.tensor_scalar(result[:], packed[:], inv_sum[:], None, op0=ALU.mult)
+        nc.vector.tensor_scalar(result[:], packed[:, 0:P], inv_sum[:], None, op0=ALU.mult)
         nc.sync.dma_start(out, result[:])

@@ -24,10 +24,10 @@ def tile_riemannianlunatemporalcompression_kernel(tc, k_store, pq, cov, v, offs,
     ):
         cov_rows = held.tile([P, COV_BLOCKS, N], F32, name="cov_rows")
         nc.sync.dma_start(cov_rows[:], cov.rearrange("(p b) j -> p b j", b=COV_BLOCKS))
-        keys = held.tile([P, S], BF16, name="keys")
-        nc.scalar.dma_start(keys[:], k_store)
         offsets = held.tile([P, N // 16], U16, name="offsets")
         nc.sync.dma_start(offsets[:], offs)
+        keys = held.tile([P, S], BF16, name="keys")
+        nc.sync.dma_start(keys[:], k_store)
         queries = held.tile([P, P], BF16, name="queries")
         nc.scalar.dma_start(queries[:], pq)
 

@@ -24,10 +24,10 @@ def tile_riemannianlunatemporalcompression_kernel(tc, k_store, pq, cov, v, offs,
     ):
         cov_rows = held.tile([P, COV_BLOCKS, N], F32, name="cov_rows")
         nc.sync.dma_start(cov_rows[:], cov.rearrange("(p b) j -> p b j", b=COV_BLOCKS))
+        keys = held.tile([P, S], BF16, name="keys")
+        nc.scalar.dma_start(keys[:], k_store)
         offsets = held.tile([P, N // 16], U16, name="offsets")
         nc.sync.dma_start(offsets[:], offs)
-        keys = held.tile([P, S], BF16, name="keys")
-        nc.sync.dma_start(keys[:], k_store)
         queries = held.tile([P, P], BF16, name="queries")
         nc.scalar.dma_start(queries[:], pq)
 
@@ -35,13 +35,16 @@ def tile_riemannianlunatemporalcompression_kernel(tc, k_store, pq, cov, v, offs,
         nc.vector.memset(ones[:], 1.0)
         identity = held.tile([P, P], F32, name="identity")
         make_identity(nc, identity[:])
+        sqrt_of_one = held.tile([P, 1], F32, name="sqrt_of_one")
+        nc.scalar.activation(sqrt_of_one[:], ones[:, 0:1], ACT.Sqrt)
 
         values_and_one = held.tile([P, P + 1], BF16, name="values_and_one")
         nc.gpsimd.dma_start(values_and_one[:, 0:P], v)
         nc.vector.memset(values_and_one[:, P : P + 1], 1.0)
 
         squares = held.tile([P, COV_BLOCKS, N], BF16, name="squares")
-        nc.vector.tensor_tensor(squares[:], cov_rows[:], cov_rows[:], ALU.mult)
+        nc.vector.tensor_tensor(squares[:, 0, :], cov_rows[:, 0, :], cov_rows[:, 0, :], ALU.mult)
+        nc.scalar.activation(squares[:, 1, :], cov_rows[:, 1, :], ACT.Square)
         sumsq = psum.tile([P, N], F32, name="sumsq")
         for b in range(COV_BLOCKS):
             nc.tensor.matmul(

@@ -12,6 +12,8 @@ S = 1024
 N = 128
 COV_BLOCKS = 2
 BETA = 0.5
+BANK = 512
+IDLE_MATMULS = 3
 
 FLOPS = 2 * P * P * N + 2 * COV_BLOCKS * P * N + 2 * P * N * P
 
@@ -31,8 +33,13 @@ def tile_riemannianlunatemporalcompression_kernel(tc, k_store, pq, cov, v, offs,
         queries = held.tile([P, P], BF16, name="queries")
         nc.scalar.dma_start(queries[:], pq)
 
-        ones = held.tile([P, P], BF16, name="ones")
+        ones = held.tile([P, BANK], BF16, name="ones")
         nc.vector.memset(ones[:], 1.0)
+
+        unread = psum.tile([P, BANK], F32, name="unread")
+
+        for repeat in range(IDLE_MATMULS):
+            nc.tensor.matmul(unread[:], ones[:, 0:P], ones[:], start=True, stop=True)
         identity = held.tile([P, P], F32, name="identity")
         make_identity(nc, identity[:])
         sqrt_of_one = held.tile([P, 1], F32, name="sqrt_of_one")
@@ -48,7 +55,7 @@ def tile_riemannianlunatemporalcompression_kernel(tc, k_store, pq, cov, v, offs,
         sumsq = psum.tile([P, N], F32, name="sumsq")
         for b in range(COV_BLOCKS):
             nc.tensor.matmul(
-                sumsq[:], ones[:], squares[:, b, :], start=(b == 0), stop=(b == COV_BLOCKS - 1)
+                sumsq[:], ones[:, 0:P], squares[:, b, :], start=(b == 0), stop=(b == COV_BLOCKS - 1)
             )
         half_dist = held.tile([P, N], F32, name="half_dist")
         nc.scalar.activation(half_dist[:], sumsq[:], ACT.Sqrt, scale=BETA * BETA)

@@ -67,13 +67,14 @@ def tile_riemannianlunatemporalcompression_kernel(tc, k_store, pq, cov, v, offs,
         nc.vector.scalar_tensor_tensor(
             z[:], score[:], 1.0 / math.sqrt(P), half_dist[:], op0=ALU.mult, op1=ALU.subtract
         )
-        row_max = held.tile([P, 1], F32, name="row_max")
-        nc.vector.tensor_reduce(row_max[:], z[:], mybir.AxisListType.X, ALU.max)
-        shifted = held.tile([P, N], F32, name="shifted")
-        nc.vector.tensor_scalar(shifted[:], z[:], row_max[:], None, op0=ALU.subtract)
+        neg_max = held.tile([P, 1], F32, name="neg_max")
+        nc.vector.tensor_reduce(neg_max[:], z[:], mybir.AxisListType.X, ALU.max, negate=True)
 
         shifted_t = psum.tile([P, P], F32, name="shifted_t")
-        nc.tensor.transpose(shifted_t[:], shifted[:], identity[:])
+        nc.tensor.matmul(shifted_t[:], z[:], identity[:], is_transpose=True, start=True, stop=False)
+        nc.tensor.matmul(
+            shifted_t[:], neg_max[:].to_broadcast([P, P]), identity[:], is_transpose=True, start=False, stop=True
+        )
         weights_t = held.tile([P, P], BF16, name="weights_t")
         nc.scalar.activation(weights_t[:], shifted_t[:], ACT.Exp)
 

@@ -52,31 +52,40 @@ def tile_riemannianlunatemporalcompression_kernel(tc, k_store, pq, cov, v, offs,
         squares = held.tile([P, COV_BLOCKS, N], BF16, name="squares")
         nc.vector.tensor_tensor(squares[:, 0, :], cov_rows[:, 0, :], cov_rows[:, 0, :], ALU.mult)
         nc.scalar.activation(squares[:, 1, :], cov_rows[:, 1, :], ACT.Square)
-        sumsq = psum.tile([P, N], F32, name="sumsq")
+        sumsq = psum.tile([P, 1], F32, name="sumsq")
         for b in range(COV_BLOCKS):
             nc.tensor.matmul(
-                sumsq[:], ones[:, 0:P], squares[:, b, :], start=(b == 0), stop=(b == COV_BLOCKS - 1)
+                sumsq[:], squares[:, b, :], ones[:, 0:1], start=(b == 0), stop=(b == COV_BLOCKS - 1)
             )
-        half_dist = held.tile([P, N], F32, name="half_dist")
-        nc.scalar.activation(half_dist[:], sumsq[:], ACT.Sqrt, scale=BETA * BETA)
+        scaled_dist = held.tile([P, 1], F32, name="scaled_dist")
+        nc.scalar.activation(scaled_dist[:], sumsq[:], ACT.Sqrt, scale=P * BETA * BETA)
+        neg_half_dist = held.tile([P, 1], F32, name="neg_half_dist")
+        nc.vector.tensor_scalar(neg_half_dist[:], scaled_dist[:], -1.0 / math.sqrt(P), None, op0=ALU.mult)
 
+        neg_queries = held.tile([P, P], BF16, name="neg_queries")
+        nc.vector.tensor_scalar(neg_queries[:], queries[:], -1.0, None, op0=ALU.mult)
+        neg_logits = psum.tile([P, N], F32, name="neg_logits")
+        nc.tensor.matmul(neg_logits[:], neg_queries[:], keys[:].indirect(offsets[:]), start=True, stop=False)
         score = psum.tile([P, N], F32, name="score")
         nc.tensor.matmul(score[:], queries[:], keys[:].indirect(offsets[:]), start=True, stop=True)
-
-        z = held.tile([P, N], F32, name="z")
-        nc.vector.scalar_tensor_tensor(
-            z[:], score[:], 1.0 / math.sqrt(P), half_dist[:], op0=ALU.mult, op1=ALU.subtract
+        nc.tensor.matmul(
+            neg_logits[:], scaled_dist[:].to_broadcast([P, P]), identity[:], is_transpose=True, start=False, stop=True
         )
-        neg_max = held.tile([P, 1], F32, name="neg_max")
-        nc.vector.tensor_reduce(neg_max[:], z[:], mybir.AxisListType.X, ALU.max, negate=True)
 
+        score_copy = held.tile([P, N], F32, name="score_copy")
+        nc.vector.tensor_copy(score_copy[:], score[:])
         shifted_t = psum.tile([P, P], F32, name="shifted_t")
-        nc.tensor.matmul(shifted_t[:], z[:], identity[:], is_transpose=True, start=True, stop=False)
+        nc.tensor.matmul(shifted_t[:], score_copy[:], identity[:], is_transpose=True, start=True, stop=False)
+        neg_max = held.tile([P, 1], F32, name="neg_max")
+        nc.vector.tensor_reduce(neg_max[:], neg_logits[:], mybir.AxisListType.X, ALU.min)
         nc.tensor.matmul(
             shifted_t[:], neg_max[:].to_broadcast([P, P]), identity[:], is_transpose=True, start=False, stop=True
         )
+
         weights_t = held.tile([P, P], BF16, name="weights_t")
-        nc.scalar.activation(weights_t[:], shifted_t[:], ACT.Exp)
+        nc.scalar.activation(
+            weights_t[:], shifted_t[:], ACT.Exp, scale=1.0 / math.sqrt(P), bias=neg_half_dist[:]
+        )
 
         packed = psum.tile([P, P + 1], F32, name="packed")
         nc.tensor.matmul(packed[:], weights_t[:], values_and_one[:], start=True, stop=True)

@@ -45,9 +45,8 @@ def tile_riemannianlunatemporalcompression_kernel(tc, k_store, pq, cov, v, offs,
         sqrt_of_one = held.tile([P, 1], F32, name="sqrt_of_one")
         nc.scalar.activation(sqrt_of_one[:], ones[:, 0:1], ACT.Sqrt)
 
-        values_and_one = held.tile([P, P + 1], BF16, name="values_and_one")
-        nc.gpsimd.dma_start(values_and_one[:, 0:P], v)
-        nc.vector.memset(values_and_one[:, P : P + 1], 1.0)
+        values = held.tile([P, P], BF16, name="values")
+        nc.gpsimd.dma_start(values[:], v)
 
         squares = held.tile([P, COV_BLOCKS, N], BF16, name="squares")
         nc.vector.tensor_tensor(squares[:, 0, :], cov_rows[:, 0, :], cov_rows[:, 0, :], ALU.mult)
@@ -87,10 +86,23 @@ def tile_riemannianlunatemporalcompression_kernel(tc, k_store, pq, cov, v, offs,
             weights_t[:], shifted_t[:], ACT.Exp, scale=1.0 / math.sqrt(P), bias=neg_half_dist[:]
         )
 
-        packed = psum.tile([P, P + 1], F32, name="packed")
-        nc.tensor.matmul(packed[:], weights_t[:], values_and_one[:], start=True, stop=True)
+        scaled_neg_max = held.tile([P, 1], F32, name="scaled_neg_max")
+        nc.vector.tensor_scalar(scaled_neg_max[:], neg_max[:], 1.0 / math.sqrt(P), None, op0=ALU.mult)
+        unread_weights = held.tile([P, N], BF16, name="unread_weights")
+        row_sum = held.tile([P, 1], F32, name="row_sum")
+        nc.scalar.activation(
+            unread_weights[:],
+            neg_logits[:],
+            ACT.Exp,
+            scale=-1.0 / math.sqrt(P),
+            bias=scaled_neg_max[:],
+            accum_out=row_sum[:],
+        )
         inv_sum = held.tile([P, 1], F32, name="inv_sum")
-        nc.vector.reciprocal(inv_sum[:], packed[:, P : P + 1])
+        nc.vector.reciprocal(inv_sum[:], row_sum[:])
+
+        packed = psum.tile([P, P], F32, name="packed")
+        nc.tensor.matmul(packed[:], weights_t[:], values[:], start=True, stop=True)
         result = held.tile([P, P], F32, name="result")
-        nc.vector.tensor_scalar(result[:], packed[:, 0:P], inv_sum[:], None, op0=ALU.mult)
+        nc.vector.tensor_scalar(result[:], packed[:], inv_sum[:], None, op0=ALU.mult)
         nc.sync.dma_start(out, result[:])

@@ -32,6 +32,8 @@ def tile_riemannianlunatemporalcompression_kernel(tc, k_store, pq, cov, v, offs,
         nc.sync.dma_start(offsets[:], offs)
         queries = held.tile([P, P], BF16, name="queries")
         nc.scalar.dma_start(queries[:], pq)
+        values = held.tile([P, P], BF16, name="values")
+        nc.sync.dma_start(values[:], v)
 
         ones = held.tile([P, BANK], BF16, name="ones")
         nc.vector.memset(ones[:], 1.0)
@@ -45,8 +47,6 @@ def tile_riemannianlunatemporalcompression_kernel(tc, k_store, pq, cov, v, offs,
         sqrt_of_one = held.tile([P, 1], F32, name="sqrt_of_one")
         nc.scalar.activation(sqrt_of_one[:], ones[:, 0:1], ACT.Sqrt)
 
-        values = held.tile([P, P], BF16, name="values")
-        nc.gpsimd.dma_start(values[:], v)
 
         squares = held.tile([P, COV_BLOCKS, N], BF16, name="squares")
         nc.vector.tensor_tensor(squares[:, 0, :], cov_rows[:, 0, :], cov_rows[:, 0, :], ALU.mult)

@@ -24,14 +24,16 @@ def tile_riemannianlunatemporalcompression_kernel(tc, k_store, pq, cov, v, offs,
         tc.tile_pool(name="held", bufs=1) as held,
         tc.psum_pool(name="psum", bufs=1) as psum,
     ):
-        cov_rows = held.tile([P, COV_BLOCKS, N], F32, name="cov_rows")
-        nc.sync.dma_start(cov_rows[:], cov.rearrange("(p b) j -> p b j", b=COV_BLOCKS))
-        keys = held.tile([P, S], BF16, name="keys")
-        nc.scalar.dma_start(keys[:], k_store)
+        cov_top = held.tile([P, N], F32, name="cov_top")
+        nc.sync.dma_start(cov_top[:], cov[0:P, :])
+        cov_bottom = held.tile([P, N], F32, name="cov_bottom")
+        nc.scalar.dma_start(cov_bottom[:], cov[P : 2 * P, :])
         offsets = held.tile([P, N // 16], U16, name="offsets")
         nc.sync.dma_start(offsets[:], offs)
         queries = held.tile([P, P], BF16, name="queries")
         nc.scalar.dma_start(queries[:], pq)
+        keys = held.tile([P, S], BF16, name="keys")
+        nc.sync.dma_start(keys[:], k_store)
         values = held.tile([P, P], BF16, name="values")
         nc.sync.dma_start(values[:], v)
 
@@ -49,8 +51,8 @@ def tile_riemannianlunatemporalcompression_kernel(tc, k_store, pq, cov, v, offs,
 
 
         squares = held.tile([P, COV_BLOCKS, N], BF16, name="squares")
-        nc.vector.tensor_tensor(squares[:, 0, :], cov_rows[:, 0, :], cov_rows[:, 0, :], ALU.mult)
-        nc.scalar.activation(squares[:, 1, :], cov_rows[:, 1, :], ACT.Square)
+        nc.vector.tensor_tensor(squares[:, 0, :], cov_top[:], cov_top[:], ALU.mult)
+        nc.scalar.activation(squares[:, 1, :], cov_bottom[:], ACT.Square)
         sumsq = psum.tile([P, 1], F32, name="sumsq")
         for b in range(COV_BLOCKS):
             nc.tensor.matmul(

@@ -12,8 +12,6 @@ S = 1024
 N = 128
 COV_BLOCKS = 2
 BETA = 0.5
-BANK = 512
-IDLE_MATMULS = 3
 
 FLOPS = 2 * P * P * N + 2 * COV_BLOCKS * P * N + 2 * P * N * P
 
@@ -37,18 +35,13 @@ def tile_riemannianlunatemporalcompression_kernel(tc, k_store, pq, cov, v, offs,
         values = held.tile([P, P], BF16, name="values")
         nc.sync.dma_start(values[:], v)
 
-        ones = held.tile([P, BANK], BF16, name="ones")
+        ones = held.tile([P, 1], BF16, name="ones")
         nc.vector.memset(ones[:], 1.0)
 
-        unread = psum.tile([P, BANK], F32, name="unread")
-
-        for repeat in range(IDLE_MATMULS):
-            nc.tensor.matmul(unread[:], ones[:, 0:P], ones[:], start=True, stop=True)
         identity = held.tile([P, P], F32, name="identity")
         make_identity(nc, identity[:])
         sqrt_of_one = held.tile([P, 1], F32, name="sqrt_of_one")
-        nc.scalar.activation(sqrt_of_one[:], ones[:, 0:1], ACT.Sqrt)
-
+        nc.scalar.activation(sqrt_of_one[:], ones[:], ACT.Sqrt)
 
         squares = held.tile([P, COV_BLOCKS, N], BF16, name="squares")
         nc.vector.tensor_tensor(squares[:, 0, :], cov_top[:], cov_top[:], ALU.mult)
@@ -56,7 +49,7 @@ def tile_riemannianlunatemporalcompression_kernel(tc, k_store, pq, cov, v, offs,
         sumsq = psum.tile([P, 1], F32, name="sumsq")
         for b in range(COV_BLOCKS):
             nc.tensor.matmul(
-                sumsq[:], squares[:, b, :], ones[:, 0:1], start=(b == 0), stop=(b == COV_BLOCKS - 1)
+                sumsq[:], squares[:, b, :], ones[:], start=(b == 0), stop=(b == COV_BLOCKS - 1)
             )
         scaled_dist = held.tile([P, 1], F32, name="scaled_dist")
         nc.scalar.activation(scaled_dist[:], sumsq[:], ACT.Sqrt, scale=P * BETA * BETA)
@@ -65,10 +58,10 @@ def tile_riemannianlunatemporalcompression_kernel(tc, k_store, pq, cov, v, offs,
 
         neg_queries = held.tile([P, P], BF16, name="neg_queries")
         nc.vector.tensor_scalar(neg_queries[:], queries[:], -1.0, None, op0=ALU.mult)
-        neg_logits = psum.tile([P, N], F32, name="neg_logits")
-        nc.tensor.matmul(neg_logits[:], neg_queries[:], keys[:].indirect(offsets[:]), start=True, stop=False)
         score = psum.tile([P, N], F32, name="score")
         nc.tensor.matmul(score[:], queries[:], keys[:].indirect(offsets[:]), start=True, stop=True)
+        neg_logits = psum.tile([P, N], F32, name="neg_logits")
+        nc.tensor.matmul(neg_logits[:], neg_queries[:], keys[:].indirect(offsets[:]), start=True, stop=False)
         nc.tensor.matmul(
             neg_logits[:], scaled_dist[:].to_broadcast([P, P]), identity[:], is_transpose=True, start=False, stop=True
         )

@@ -45,7 +45,7 @@ def tile_riemannianlunatemporalcompression_kernel(tc, k_store, pq, cov, v, offs,
 
         squares = held.tile([P, COV_BLOCKS, N], BF16, name="squares")
         nc.vector.tensor_tensor(squares[:, 0, :], cov_top[:], cov_top[:], ALU.mult)
-        nc.scalar.activation(squares[:, 1, :], cov_bottom[:], ACT.Square)
+        nc.vector.tensor_tensor(squares[:, 1, :], cov_bottom[:], cov_bottom[:], ALU.mult)
         sumsq = psum.tile([P, 1], F32, name="sumsq")
         for b in range(COV_BLOCKS):
             nc.tensor.matmul(

@@ -26,12 +26,12 @@ def tile_riemannianlunatemporalcompression_kernel(tc, k_store, pq, cov, v, offs,
         nc.sync.dma_start(cov_top[:], cov[0:P, :])
         cov_bottom = held.tile([P, N], F32, name="cov_bottom")
         nc.scalar.dma_start(cov_bottom[:], cov[P : 2 * P, :])
+        keys = held.tile([P, S], BF16, name="keys")
+        nc.scalar.dma_start(keys[:], k_store)
+        queries = held.tile([P, P], BF16, name="queries")
+        nc.sync.dma_start(queries[:], pq)
         offsets = held.tile([P, N // 16], U16, name="offsets")
         nc.sync.dma_start(offsets[:], offs)
-        queries = held.tile([P, P], BF16, name="queries")
-        nc.scalar.dma_start(queries[:], pq)
-        keys = held.tile([P, S], BF16, name="keys")
-        nc.sync.dma_start(keys[:], k_store)
         values = held.tile([P, P], BF16, name="values")
         nc.sync.dma_start(values[:], v)
 
@@ -57,7 +57,7 @@ def tile_riemannianlunatemporalcompression_kernel(tc, k_store, pq, cov, v, offs,
         nc.vector.tensor_scalar(neg_half_dist[:], scaled_dist[:], -1.0 / math.sqrt(P), None, op0=ALU.mult)
 
         neg_queries = held.tile([P, P], BF16, name="neg_queries")
-        nc.vector.tensor_scalar(neg_queries[:], queries[:], -1.0, None, op0=ALU.mult)
+        nc.scalar.activation(neg_queries[:], queries[:], ACT.Copy, scale=-1.0)
         score = psum.tile([P, N], F32, name="score")
         nc.tensor.matmul(score[:], queries[:], keys[:].indirect(offsets[:]), start=True, stop=True)
         neg_logits = psum.tile([P, N], F32, name="neg_logits")

@@ -96,8 +96,12 @@ def tile_riemannianlunatemporalcompression_kernel(tc, k_store, pq, cov, v, offs,
         inv_sum = held.tile([P, 1], F32, name="inv_sum")
         nc.vector.reciprocal(inv_sum[:], row_sum[:])
 
-        packed = psum.tile([P, P], F32, name="packed")
-        nc.tensor.matmul(packed[:], weights_t[:], values[:], start=True, stop=True)
         result = held.tile([P, P], F32, name="result")
-        nc.vector.tensor_scalar(result[:], packed[:], inv_sum[:], None, op0=ALU.mult)
+        left, right = slice(0, P // 2), slice(P // 2, P)
+        packed_left = psum.tile([P, P // 2], F32, name="packed_left")
+        nc.tensor.matmul(packed_left[:], weights_t[:], values[:, left], start=True, stop=True)
+        nc.vector.tensor_scalar(result[:, left], packed_left[:], inv_sum[:], None, op0=ALU.mult)
+        packed_right = psum.tile([P, P // 2], F32, name="packed_right")
+        nc.tensor.matmul(packed_right[:], weights_t[:], values[:, right], start=True, stop=True)
+        nc.scalar.activation(result[:, right], packed_right[:], ACT.Copy, scale=inv_sum[:])
         nc.sync.dma_start(out, result[:])

import math

import concourse.mybir as mybir
from concourse.masks import make_identity

BF16, F32, U16 = mybir.dt.bfloat16, mybir.dt.float32, mybir.dt.uint16
ALU = mybir.AluOpType
ACT = mybir.ActivationFunctionType

P = 128
S = 1024
N = 128
COV_BLOCKS = 2
BETA = 0.5

FLOPS = 2 * P * P * N + 2 * COV_BLOCKS * P * N + 2 * P * N * P


def tile_riemannianlunatemporalcompression_kernel(tc, k_store, pq, cov, v, offs, out):
    nc = tc.nc
    with (
        tc.tile_pool(name="held", bufs=1) as held,
        tc.psum_pool(name="psum", bufs=1) as psum,
    ):
        cov_top = held.tile([P, N], F32, name="cov_top")
        nc.sync.dma_start(cov_top[:], cov[0:P, :])
        cov_bottom = held.tile([P, N], F32, name="cov_bottom")
        nc.scalar.dma_start(cov_bottom[:], cov[P : 2 * P, :])
        keys = held.tile([P, S], BF16, name="keys")
        nc.scalar.dma_start(keys[:], k_store)
        queries = held.tile([P, P], BF16, name="queries")
        nc.sync.dma_start(queries[:], pq)
        offsets = held.tile([P, N // 16], U16, name="offsets")
        nc.sync.dma_start(offsets[:], offs)
        values = held.tile([P, P], BF16, name="values")
        nc.sync.dma_start(values[:], v)

        ones = held.tile([P, 1], BF16, name="ones")
        nc.vector.memset(ones[:], 1.0)

        identity = held.tile([P, P], F32, name="identity")
        make_identity(nc, identity[:])
        sqrt_of_one = held.tile([P, 1], F32, name="sqrt_of_one")
        nc.scalar.activation(sqrt_of_one[:], ones[:], ACT.Sqrt)

        squares = held.tile([P, COV_BLOCKS, N], BF16, name="squares")
        nc.vector.tensor_tensor(squares[:, 0, :], cov_top[:], cov_top[:], ALU.mult)
        nc.vector.tensor_tensor(squares[:, 1, :], cov_bottom[:], cov_bottom[:], ALU.mult)
        sumsq = psum.tile([P, 1], F32, name="sumsq")
        for b in range(COV_BLOCKS):
            nc.tensor.matmul(
                sumsq[:], squares[:, b, :], ones[:], start=(b == 0), stop=(b == COV_BLOCKS - 1)
            )
        scaled_dist = held.tile([P, 1], F32, name="scaled_dist")
        nc.scalar.activation(scaled_dist[:], sumsq[:], ACT.Sqrt, scale=P * BETA * BETA)
        neg_half_dist = held.tile([P, 1], F32, name="neg_half_dist")
        nc.vector.tensor_scalar(neg_half_dist[:], scaled_dist[:], -1.0 / math.sqrt(P), None, op0=ALU.mult)

        neg_queries = held.tile([P, P], BF16, name="neg_queries")
        nc.scalar.activation(neg_queries[:], queries[:], ACT.Copy, scale=-1.0)
        score = psum.tile([P, N], F32, name="score")
        nc.tensor.matmul(score[:], queries[:], keys[:].indirect(offsets[:]), start=True, stop=True)
        neg_logits = psum.tile([P, N], F32, name="neg_logits")
        nc.tensor.matmul(neg_logits[:], neg_queries[:], keys[:].indirect(offsets[:]), start=True, stop=False)
        nc.tensor.matmul(
            neg_logits[:], scaled_dist[:].to_broadcast([P, P]), identity[:], is_transpose=True, start=False, stop=True
        )

        score_copy = held.tile([P, N], F32, name="score_copy")
        nc.vector.tensor_copy(score_copy[:], score[:])
        shifted_t = psum.tile([P, P], F32, name="shifted_t")
        nc.tensor.matmul(shifted_t[:], score_copy[:], identity[:], is_transpose=True, start=True, stop=False)
        neg_max = held.tile([P, 1], F32, name="neg_max")
        nc.vector.tensor_reduce(neg_max[:], neg_logits[:], mybir.AxisListType.X, ALU.min)
        nc.tensor.matmul(
            shifted_t[:], neg_max[:].to_broadcast([P, P]), identity[:], is_transpose=True, start=False, stop=True
        )

        weights_t = held.tile([P, P], BF16, name="weights_t")
        nc.scalar.activation(
            weights_t[:], shifted_t[:], ACT.Exp, scale=1.0 / math.sqrt(P), bias=neg_half_dist[:]
        )

        scaled_neg_max = held.tile([P, 1], F32, name="scaled_neg_max")
        nc.vector.tensor_scalar(scaled_neg_max[:], neg_max[:], 1.0 / math.sqrt(P), None, op0=ALU.mult)
        unread_weights = held.tile([P, N], BF16, name="unread_weights")
        row_sum = held.tile([P, 1], F32, name="row_sum")
        nc.scalar.activation(
            unread_weights[:],
            neg_logits[:],
            ACT.Exp,
            scale=-1.0 / math.sqrt(P),
            bias=scaled_neg_max[:],
            accum_out=row_sum[:],
        )
        inv_sum = held.tile([P, 1], F32, name="inv_sum")
        nc.vector.reciprocal(inv_sum[:], row_sum[:])

        result = held.tile([P, P], F32, name="result")
        left, right = slice(0, P // 2), slice(P // 2, P)
        packed_left = psum.tile([P, P // 2], F32, name="packed_left")
        nc.tensor.matmul(packed_left[:], weights_t[:], values[:, left], start=True, stop=True)
        nc.vector.tensor_scalar(result[:, left], packed_left[:], inv_sum[:], None, op0=ALU.mult)
        packed_right = psum.tile([P, P // 2], F32, name="packed_right")
        nc.tensor.matmul(packed_right[:], weights_t[:], values[:, right], start=True, stop=True)
        nc.scalar.activation(result[:, right], packed_right[:], ACT.Copy, scale=inv_sum[:])
        nc.sync.dma_start(out, result[:])
